import numpy as np
import ml_dtypes

BF16 = ml_dtypes.bfloat16


def bf(x):
    return np.asarray(x, np.float32).astype(BF16)


def f32(x):
    return np.asarray(x, np.float32)


def f64(x):
    return np.asarray(x).astype(np.float64)


def striped(idx):
    return np.tile(idx.reshape(-1, 16).T, (8, 1))


C, S, K, H, N = 128, 256, 32, 128, 4096


def setup_inputs():
    return {"x": f32(np.random.standard_normal((K, C, S))), "scores": f32(np.random.standard_normal((C, N))), "offs": striped(np.concatenate([np.random.permutation(S)[:H] for _ in range(K)]))}


def reference(x, scores, offs):
    idx = offs[:16].T.reshape(-1)
    xx = f64(x)
    z = np.stack([xx[t][:, idx[t * H:(t + 1) * H]] for t in range(K)], axis=1) + f64(scores).reshape(C, K, H)
    e = np.exp(z - z.max(axis=-1, keepdims=True))
    return (e / e.sum(axis=-1, keepdims=True)).reshape(C, N)

@@ -1,0 +1,83 @@
+import concourse.mybir as mybir
+
+F32 = mybir.dt.float32
+U16 = mybir.dt.uint16
+ADD = mybir.AluOpType.add
+MAX = mybir.AluOpType.max
+EXP = mybir.ActivationFunctionType.Exp
+COPY = mybir.ActivationFunctionType.Copy
+X_AXIS = mybir.AxisListType.X
+
+ROWS = 128
+BUCKETS = 256
+QUERIES = 32
+KEYS = 128
+OFFSET_COLS = KEYS // 16
+GROUP = 4
+GROUPS = QUERIES // GROUP
+WIDTH = GROUP * KEYS
+
+
+def tile_ngrammultiheadattention_kernel(tc, x, scores, offs, out):
+    nc = tc.nc
+    with (
+        tc.tile_pool(name="held", bufs=1) as held,
+        tc.tile_pool(name="work", bufs=1) as work,
+    ):
+        offsets = held.tile([ROWS, QUERIES * OFFSET_COLS], U16, name="offsets")
+        nc.sync.dma_start(offsets[:], offs)
+
+        tables = []
+        addends = []
+        for g in range(GROUPS):
+            addend = work.tile([ROWS, WIDTH], F32, name=f"addend{g}")
+            nc.scalar.dma_start(addend[:], scores[:, g * WIDTH : (g + 1) * WIDTH])
+            addends.append(addend)
+            for t in range(g * GROUP, (g + 1) * GROUP):
+                table = work.tile([ROWS, BUCKETS], F32, name=f"table{t}")
+                nc.sync.dma_start(table[:], x[t, :, :])
+                tables.append(table)
+
+        for g in range(GROUPS):
+            logits = work.tile([ROWS, WIDTH], F32, name=f"logits{g}")
+            powers = work.tile([ROWS, WIDTH], F32, name=f"powers{g}")
+            probs = work.tile([ROWS, WIDTH], F32, name=f"probs{g}")
+            neg_max = work.tile([ROWS, GROUP], F32, name=f"neg_max{g}")
+            sums = work.tile([ROWS, GROUP], F32, name=f"sums{g}")
+            inv_sums = work.tile([ROWS, GROUP], F32, name=f"inv_sums{g}")
+
+            for i in range(GROUP):
+                t = g * GROUP + i
+                keys = slice(i * KEYS, (i + 1) * KEYS)
+                piece = offsets[:, t * OFFSET_COLS : (t + 1) * OFFSET_COLS]
+                nc.vector.tensor_tensor(
+                    logits[:, keys], tables[t][:].indirect(piece), addends[g][:, keys], ADD
+                )
+
+            nc.vector.tensor_reduce(
+                neg_max[:],
+                logits[:].rearrange("c (q k) -> c q k", k=KEYS),
+                X_AXIS,
+                MAX,
+                negate=True,
+            )
+
+            for i in range(GROUP):
+                keys = slice(i * KEYS, (i + 1) * KEYS)
+                nc.scalar.activation(
+                    powers[:, keys],
+                    logits[:, keys],
+                    EXP,
+                    bias=neg_max[:, i : i + 1],
+                    accum_out=sums[:, i : i + 1],
+                )
+
+            nc.vector.reciprocal(inv_sums[:], sums[:])
+
+            for i in range(GROUP):
+                keys = slice(i * KEYS, (i + 1) * KEYS)
+                nc.scalar.activation(
+                    probs[:, keys], powers[:, keys], COPY, scale=inv_sums[:, i : i + 1]
+                )
+
+            nc.sync.dma_start(out[:, g * WIDTH : (g + 1) * WIDTH], probs[:])

@@ -38,13 +38,12 @@ def tile_ngrammultiheadattention_kernel(tc, x, scores, offs, out):
                 nc.sync.dma_start(table[:], x[t, :, :])
                 tables.append(table)
 
-        for g in range(GROUPS):
+        powers = [work.tile([ROWS, WIDTH], F32, name=f"powers{g}") for g in range(GROUPS)]
+        sums = [work.tile([ROWS, GROUP], F32, name=f"sums{g}") for g in range(GROUPS)]
+
+        def exponentials(g):
             logits = work.tile([ROWS, WIDTH], F32, name=f"logits{g}")
-            powers = work.tile([ROWS, WIDTH], F32, name=f"powers{g}")
-            probs = work.tile([ROWS, WIDTH], F32, name=f"probs{g}")
             neg_max = work.tile([ROWS, GROUP], F32, name=f"neg_max{g}")
-            sums = work.tile([ROWS, GROUP], F32, name=f"sums{g}")
-            inv_sums = work.tile([ROWS, GROUP], F32, name=f"inv_sums{g}")
 
             for i in range(GROUP):
                 t = g * GROUP + i
@@ -65,19 +64,26 @@ def tile_ngrammultiheadattention_kernel(tc, x, scores, offs, out):
             for i in range(GROUP):
                 keys = slice(i * KEYS, (i + 1) * KEYS)
                 nc.scalar.activation(
-                    powers[:, keys],
+                    powers[g][:, keys],
                     logits[:, keys],
                     EXP,
                     bias=neg_max[:, i : i + 1],
-                    accum_out=sums[:, i : i + 1],
+                    accum_out=sums[g][:, i : i + 1],
                 )
 
-            nc.vector.reciprocal(inv_sums[:], sums[:])
-
+        def normalise(g):
+            probs = work.tile([ROWS, WIDTH], F32, name=f"probs{g}")
+            inv_sums = work.tile([ROWS, GROUP], F32, name=f"inv_sums{g}")
+            nc.vector.reciprocal(inv_sums[:], sums[g][:])
             for i in range(GROUP):
                 keys = slice(i * KEYS, (i + 1) * KEYS)
                 nc.scalar.activation(
-                    probs[:, keys], powers[:, keys], COPY, scale=inv_sums[:, i : i + 1]
+                    probs[:, keys], powers[g][:, keys], COPY, scale=inv_sums[:, i : i + 1]
                 )
-
             nc.sync.dma_start(out[:, g * WIDTH : (g + 1) * WIDTH], probs[:])
+
+        for g in range(GROUPS):
+            exponentials(g)
+            if g > 0:
+                normalise(g - 1)
+        normalise(GROUPS - 1)

@@ -13,13 +13,14 @@ BUCKETS = 256
 QUERIES = 32
 KEYS = 128
 OFFSET_COLS = KEYS // 16
-GROUP = 4
-GROUPS = QUERIES // GROUP
-WIDTH = GROUP * KEYS
+
+GROUP_SIZES = (8, 8, 8, 4, 2, 1, 1)
+assert sum(GROUP_SIZES) == QUERIES
 
 
 def tile_ngrammultiheadattention_kernel(tc, x, scores, offs, out):
     nc = tc.nc
+    first_query = [sum(GROUP_SIZES[:g]) for g in range(len(GROUP_SIZES))]
     with (
         tc.tile_pool(name="held", bufs=1) as held,
         tc.tile_pool(name="work", bufs=1) as work,
@@ -29,24 +30,27 @@ def tile_ngrammultiheadattention_kernel(tc, x, scores, offs, out):
 
         tables = []
         addends = []
-        for g in range(GROUPS):
-            addend = work.tile([ROWS, WIDTH], F32, name=f"addend{g}")
-            nc.scalar.dma_start(addend[:], scores[:, g * WIDTH : (g + 1) * WIDTH])
+        for g, size in enumerate(GROUP_SIZES):
+            columns = slice(first_query[g] * KEYS, (first_query[g] + size) * KEYS)
+            addend = work.tile([ROWS, size * KEYS], F32, name=f"addend{g}")
+            nc.scalar.dma_start(addend[:], scores[:, columns])
             addends.append(addend)
-            for t in range(g * GROUP, (g + 1) * GROUP):
+            for t in range(first_query[g], first_query[g] + size):
                 table = work.tile([ROWS, BUCKETS], F32, name=f"table{t}")
                 nc.sync.dma_start(table[:], x[t, :, :])
                 tables.append(table)
 
-        powers = [work.tile([ROWS, WIDTH], F32, name=f"powers{g}") for g in range(GROUPS)]
-        sums = [work.tile([ROWS, GROUP], F32, name=f"sums{g}") for g in range(GROUPS)]
+        for g, size in enumerate(GROUP_SIZES):
+            columns = slice(first_query[g] * KEYS, (first_query[g] + size) * KEYS)
+            logits = work.tile([ROWS, size * KEYS], F32, name=f"logits{g}")
+            powers = work.tile([ROWS, size * KEYS], F32, name=f"powers{g}")
+            probs = work.tile([ROWS, size * KEYS], F32, name=f"probs{g}")
+            neg_max = work.tile([ROWS, size], F32, name=f"neg_max{g}")
+            sums = work.tile([ROWS, size], F32, name=f"sums{g}")
+            inv_sums = work.tile([ROWS, size], F32, name=f"inv_sums{g}")
 
-        def exponentials(g):
-            logits = work.tile([ROWS, WIDTH], F32, name=f"logits{g}")
-            neg_max = work.tile([ROWS, GROUP], F32, name=f"neg_max{g}")
-
-            for i in range(GROUP):
-                t = g * GROUP + i
+            for i in range(size):
+                t = first_query[g] + i
                 keys = slice(i * KEYS, (i + 1) * KEYS)
                 piece = offsets[:, t * OFFSET_COLS : (t + 1) * OFFSET_COLS]
                 nc.vector.tensor_tensor(
@@ -61,29 +65,22 @@ def tile_ngrammultiheadattention_kernel(tc, x, scores, offs, out):
                 negate=True,
             )
 
-            for i in range(GROUP):
+            for i in range(size):
                 keys = slice(i * KEYS, (i + 1) * KEYS)
                 nc.scalar.activation(
-                    powers[g][:, keys],
+                    powers[:, keys],
                     logits[:, keys],
                     EXP,
                     bias=neg_max[:, i : i + 1],
-                    accum_out=sums[g][:, i : i + 1],
+                    accum_out=sums[:, i : i + 1],
                 )
 
-        def normalise(g):
-            probs = work.tile([ROWS, WIDTH], F32, name=f"probs{g}")
-            inv_sums = work.tile([ROWS, GROUP], F32, name=f"inv_sums{g}")
-            nc.vector.reciprocal(inv_sums[:], sums[g][:])
-            for i in range(GROUP):
+            nc.vector.reciprocal(inv_sums[:], sums[:])
+
+            for i in range(size):
                 keys = slice(i * KEYS, (i + 1) * KEYS)
                 nc.scalar.activation(
-                    probs[:, keys], powers[g][:, keys], COPY, scale=inv_sums[:, i : i + 1]
+                    probs[:, keys], powers[:, keys], COPY, scale=inv_sums[:, i : i + 1]
                 )
-            nc.sync.dma_start(out[:, g * WIDTH : (g + 1) * WIDTH], probs[:])
 
-        for g in range(GROUPS):
-            exponentials(g)
-            if g > 0:
-                normalise(g - 1)
-        normalise(GROUPS - 1)
+            nc.sync.dma_start(out[:, columns], probs[:])

@@ -83,4 +83,4 @@ def tile_ngrammultiheadattention_kernel(tc, x, scores, offs, out):
                     probs[:, keys], powers[:, keys], COPY, scale=inv_sums[:, i : i + 1]
                 )
 
-            nc.sync.dma_start(out[:, columns], probs[:])
+            nc.gpsimd.dma_start(out[:, columns], probs[:])

@@ -17,6 +17,9 @@ OFFSET_COLS = KEYS // 16
 GROUP_SIZES = (8, 8, 8, 4, 2, 1, 1)
 assert sum(GROUP_SIZES) == QUERIES
 
+LOAD_SIZES = (1, 1, 2, 4, 8, 8, 4, 2, 1, 1)
+assert sum(LOAD_SIZES) == QUERIES
+
 
 def tile_ngrammultiheadattention_kernel(tc, x, scores, offs, out):
     nc = tc.nc
@@ -30,14 +33,14 @@ def tile_ngrammultiheadattention_kernel(tc, x, scores, offs, out):
 
         tables = []
         addends = []
-        for g, size in enumerate(GROUP_SIZES):
-            columns = slice(first_query[g] * KEYS, (first_query[g] + size) * KEYS)
-            addend = work.tile([ROWS, size * KEYS], F32, name=f"addend{g}")
-            nc.scalar.dma_start(addend[:], scores[:, columns])
-            addends.append(addend)
-            for t in range(first_query[g], first_query[g] + size):
-                table = work.tile([ROWS, BUCKETS], F32, name=f"table{t}")
-                nc.sync.dma_start(table[:], x[t, :, :])
+        for size in LOAD_SIZES:
+            t0 = len(tables)
+            loaded = work.tile([ROWS, size * KEYS], F32, name=f"scores{t0}")
+            nc.sync.dma_start(loaded[:], scores[:, t0 * KEYS : (t0 + size) * KEYS])
+            for i in range(size):
+                addends.append(loaded[:, i * KEYS : (i + 1) * KEYS])
+                table = work.tile([ROWS, BUCKETS], F32, name=f"table{t0 + i}")
+                nc.sync.dma_start(table[:], x[t0 + i, :, :])
                 tables.append(table)
 
         for g, size in enumerate(GROUP_SIZES):
@@ -54,7 +57,7 @@ def tile_ngrammultiheadattention_kernel(tc, x, scores, offs, out):
                 keys = slice(i * KEYS, (i + 1) * KEYS)
                 piece = offsets[:, t * OFFSET_COLS : (t + 1) * OFFSET_COLS]
                 nc.vector.tensor_tensor(
-                    logits[:, keys], tables[t][:].indirect(piece), addends[g][:, keys], ADD
+                    logits[:, keys], tables[t][:].indirect(piece), addends[t], ADD
                 )
 
             nc.vector.tensor_reduce(
@@ -83,4 +86,4 @@ def tile_ngrammultiheadattention_kernel(tc, x, scores, offs, out):
                     probs[:, keys], powers[:, keys], COPY, scale=inv_sums[:, i : i + 1]
                 )
 
-            nc.gpsimd.dma_start(out[:, columns], probs[:])
+            nc.sync.dma_start(out[:, columns], probs[:])

@@ -17,13 +17,14 @@ OFFSET_COLS = KEYS // 16
 GROUP_SIZES = (8, 8, 8, 4, 2, 1, 1)
 assert sum(GROUP_SIZES) == QUERIES
 
-LOAD_SIZES = (1, 1, 2, 4, 8, 8, 4, 2, 1, 1)
-assert sum(LOAD_SIZES) == QUERIES
+PIECE_STARTS = (0, 1, 2, 4, 8, 15, 23, 27, 29)
 
 
 def tile_ngrammultiheadattention_kernel(tc, x, scores, offs, out):
     nc = tc.nc
     first_query = [sum(GROUP_SIZES[:g]) for g in range(len(GROUP_SIZES))]
+    last_query = [first_query[g] + GROUP_SIZES[g] - 1 for g in range(len(GROUP_SIZES))]
+    piece_ends = PIECE_STARTS[1:] + (QUERIES,)
     with (
         tc.tile_pool(name="held", bufs=1) as held,
         tc.tile_pool(name="work", bufs=1) as work,
@@ -33,15 +34,21 @@ def tile_ngrammultiheadattention_kernel(tc, x, scores, offs, out):
 
         tables = []
         addends = []
-        for size in LOAD_SIZES:
-            t0 = len(tables)
-            loaded = work.tile([ROWS, size * KEYS], F32, name=f"scores{t0}")
-            nc.sync.dma_start(loaded[:], scores[:, t0 * KEYS : (t0 + size) * KEYS])
-            for i in range(size):
+
+        def load_piece(t0, t1):
+            loaded = work.tile([ROWS, (t1 - t0) * KEYS], F32, name=f"scores{t0}")
+            nc.sync.dma_start(loaded[:], scores[:, t0 * KEYS : t1 * KEYS])
+            for i in range(t1 - t0):
                 addends.append(loaded[:, i * KEYS : (i + 1) * KEYS])
-                table = work.tile([ROWS, BUCKETS], F32, name=f"table{t0 + i}")
-                nc.sync.dma_start(table[:], x[t0 + i, :, :])
-                tables.append(table)
+
+        for t in range(QUERIES):
+            if t in PIECE_STARTS and t not in last_query:
+                load_piece(t, piece_ends[PIECE_STARTS.index(t)])
+            table = work.tile([ROWS, BUCKETS], F32, name=f"table{t}")
+            nc.sync.dma_start(table[:], x[t, :, :])
+            tables.append(table)
+            if t - 1 in PIECE_STARTS and t - 1 in last_query:
+                load_piece(t - 1, piece_ends[PIECE_STARTS.index(t - 1)])
 
         for g, size in enumerate(GROUP_SIZES):
             columns = slice(first_query[g] * KEYS, (first_query[g] + size) * KEYS)

@@ -14,16 +14,15 @@ QUERIES = 32
 KEYS = 128
 OFFSET_COLS = KEYS // 16
 
-GROUP_SIZES = (8, 8, 8, 4, 2, 1, 1)
+GROUP_SIZES = (4, 4, 4, 4, 4, 4, 4, 2, 1, 1)
 assert sum(GROUP_SIZES) == QUERIES
+FIRST_QUERY = [sum(GROUP_SIZES[:g]) for g in range(len(GROUP_SIZES))]
 
-PIECE_STARTS = (0, 1, 2, 4, 8, 15, 23, 27, 29)
+PIECE_STARTS = (0, 1, 2, 4, 8, 16, 24)
 
 
 def tile_ngrammultiheadattention_kernel(tc, x, scores, offs, out):
     nc = tc.nc
-    first_query = [sum(GROUP_SIZES[:g]) for g in range(len(GROUP_SIZES))]
-    last_query = [first_query[g] + GROUP_SIZES[g] - 1 for g in range(len(GROUP_SIZES))]
     piece_ends = PIECE_STARTS[1:] + (QUERIES,)
     with (
         tc.tile_pool(name="held", bufs=1) as held,
@@ -34,37 +33,35 @@ def tile_ngrammultiheadattention_kernel(tc, x, scores, offs, out):
 
         tables = []
         addends = []
-
-        def load_piece(t0, t1):
-            loaded = work.tile([ROWS, (t1 - t0) * KEYS], F32, name=f"scores{t0}")
-            nc.sync.dma_start(loaded[:], scores[:, t0 * KEYS : t1 * KEYS])
-            for i in range(t1 - t0):
-                addends.append(loaded[:, i * KEYS : (i + 1) * KEYS])
-
         for t in range(QUERIES):
-            if t in PIECE_STARTS and t not in last_query:
-                load_piece(t, piece_ends[PIECE_STARTS.index(t)])
+            if t in PIECE_STARTS:
+                t_end = piece_ends[PIECE_STARTS.index(t)]
+                loaded = work.tile([ROWS, (t_end - t) * KEYS], F32, name=f"scores{t}")
+                nc.sync.dma_start(loaded[:], scores[:, t * KEYS : t_end * KEYS])
+                for i in range(t_end - t):
+                    addends.append(loaded[:, i * KEYS : (i + 1) * KEYS])
             table = work.tile([ROWS, BUCKETS], F32, name=f"table{t}")
             nc.sync.dma_start(table[:], x[t, :, :])
             tables.append(table)
-            if t - 1 in PIECE_STARTS and t - 1 in last_query:
-                load_piece(t - 1, piece_ends[PIECE_STARTS.index(t - 1)])
 
-        for g, size in enumerate(GROUP_SIZES):
-            columns = slice(first_query[g] * KEYS, (first_query[g] + size) * KEYS)
+        powers = []
+        sums = []
+
+        def start_group(g):
+            size = GROUP_SIZES[g]
             logits = work.tile([ROWS, size * KEYS], F32, name=f"logits{g}")
-            powers = work.tile([ROWS, size * KEYS], F32, name=f"powers{g}")
-            probs = work.tile([ROWS, size * KEYS], F32, name=f"probs{g}")
             neg_max = work.tile([ROWS, size], F32, name=f"neg_max{g}")
-            sums = work.tile([ROWS, size], F32, name=f"sums{g}")
-            inv_sums = work.tile([ROWS, size], F32, name=f"inv_sums{g}")
+            powers.append(work.tile([ROWS, size * KEYS], F32, name=f"powers{g}"))
+            sums.append(work.tile([ROWS, size], F32, name=f"sums{g}"))
 
             for i in range(size):
-                t = first_query[g] + i
-                keys = slice(i * KEYS, (i + 1) * KEYS)
+                t = FIRST_QUERY[g] + i
                 piece = offsets[:, t * OFFSET_COLS : (t + 1) * OFFSET_COLS]
                 nc.vector.tensor_tensor(
-                    logits[:, keys], tables[t][:].indirect(piece), addends[t], ADD
+                    logits[:, i * KEYS : (i + 1) * KEYS],
+                    tables[t][:].indirect(piece),
+                    addends[t],
+                    ADD,
                 )
 
             nc.vector.tensor_reduce(
@@ -78,19 +75,32 @@ def tile_ngrammultiheadattention_kernel(tc, x, scores, offs, out):
             for i in range(size):
                 keys = slice(i * KEYS, (i + 1) * KEYS)
                 nc.scalar.activation(
-                    powers[:, keys],
+                    powers[g][:, keys],
                     logits[:, keys],
                     EXP,
                     bias=neg_max[:, i : i + 1],
-                    accum_out=sums[:, i : i + 1],
+                    accum_out=sums[g][:, i : i + 1],
                 )
 
-            nc.vector.reciprocal(inv_sums[:], sums[:])
-
+        def finish_group(g):
+            size = GROUP_SIZES[g]
+            probs = work.tile([ROWS, size * KEYS], F32, name=f"probs{g}")
+            if g + 1 < len(GROUP_SIZES):
+                freed = FIRST_QUERY[g + 1] + GROUP_SIZES[g + 1] - 1
+                inv_sums = work.tile([ROWS, size], F32, name=f"inv_sums{g}", tag=f"table{freed}")
+            else:
+                inv_sums = work.tile([ROWS, size], F32, name=f"inv_sums{g}")
+            nc.vector.reciprocal(inv_sums[:], sums[g][:])
             for i in range(size):
                 keys = slice(i * KEYS, (i + 1) * KEYS)
                 nc.scalar.activation(
-                    probs[:, keys], powers[:, keys], COPY, scale=inv_sums[:, i : i + 1]
+                    probs[:, keys], powers[g][:, keys], COPY, scale=inv_sums[:, i : i + 1]
                 )
-
+            columns = slice(FIRST_QUERY[g] * KEYS, (FIRST_QUERY[g] + size) * KEYS)
             nc.sync.dma_start(out[:, columns], probs[:])
+
+        for g in range(len(GROUP_SIZES)):
+            start_group(g)
+            if g > 0:
+                finish_group(g - 1)
+        finish_group(len(GROUP_SIZES) - 1)

@@ -14,11 +14,13 @@ QUERIES = 32
 KEYS = 128
 OFFSET_COLS = KEYS // 16
 
-GROUP_SIZES = (4, 4, 4, 4, 4, 4, 4, 2, 1, 1)
+GROUP_SIZES = (5, 5, 5, 5, 5, 3, 2, 1, 1)
 assert sum(GROUP_SIZES) == QUERIES
-FIRST_QUERY = [sum(GROUP_SIZES[:g]) for g in range(len(GROUP_SIZES))]
+FIRST_QUERY = [sum(GROUP_SIZES[:g]) for g in range(len(GROUP_SIZES) + 1)]
 
-PIECE_STARTS = (0, 1, 2, 4, 8, 16, 24)
+FIRST_SCALED_BY_VECTOR = 6
+
+PIECE_STARTS = (0, 2, 5, 13, 21, 29)
 
 
 def tile_ngrammultiheadattention_kernel(tc, x, scores, offs, out):
@@ -44,63 +46,66 @@ def tile_ngrammultiheadattention_kernel(tc, x, scores, offs, out):
             nc.sync.dma_start(table[:], x[t, :, :])
             tables.append(table)
 
+        logits = []
         powers = []
         sums = []
-
-        def start_group(g):
-            size = GROUP_SIZES[g]
-            logits = work.tile([ROWS, size * KEYS], F32, name=f"logits{g}")
-            neg_max = work.tile([ROWS, size], F32, name=f"neg_max{g}")
+        for g, size in enumerate(GROUP_SIZES):
+            logits.append(work.tile([ROWS, size * KEYS], F32, name=f"logits{g}"))
             powers.append(work.tile([ROWS, size * KEYS], F32, name=f"powers{g}"))
             sums.append(work.tile([ROWS, size], F32, name=f"sums{g}"))
 
-            for i in range(size):
-                t = FIRST_QUERY[g] + i
-                piece = offsets[:, t * OFFSET_COLS : (t + 1) * OFFSET_COLS]
-                nc.vector.tensor_tensor(
-                    logits[:, i * KEYS : (i + 1) * KEYS],
-                    tables[t][:].indirect(piece),
-                    addends[t],
-                    ADD,
-                )
+        def gather(g, t):
+            i = t - FIRST_QUERY[g]
+            piece = offsets[:, t * OFFSET_COLS : (t + 1) * OFFSET_COLS]
+            nc.vector.tensor_tensor(
+                logits[g][:, i * KEYS : (i + 1) * KEYS],
+                tables[t][:].indirect(piece),
+                addends[t],
+                ADD,
+            )
 
+        def exponentials(g):
+            neg_max = work.tile([ROWS, GROUP_SIZES[g]], F32, name=f"neg_max{g}")
             nc.vector.tensor_reduce(
                 neg_max[:],
-                logits[:].rearrange("c (q k) -> c q k", k=KEYS),
+                logits[g][:].rearrange("c (q k) -> c q k", k=KEYS),
                 X_AXIS,
                 MAX,
                 negate=True,
             )
-
-            for i in range(size):
+            for i in range(GROUP_SIZES[g]):
                 keys = slice(i * KEYS, (i + 1) * KEYS)
                 nc.scalar.activation(
                     powers[g][:, keys],
-                    logits[:, keys],
+                    logits[g][:, keys],
                     EXP,
                     bias=neg_max[:, i : i + 1],
                     accum_out=sums[g][:, i : i + 1],
                 )
 
-        def finish_group(g):
-            size = GROUP_SIZES[g]
-            probs = work.tile([ROWS, size * KEYS], F32, name=f"probs{g}")
-            if g + 1 < len(GROUP_SIZES):
-                freed = FIRST_QUERY[g + 1] + GROUP_SIZES[g + 1] - 1
-                inv_sums = work.tile([ROWS, size], F32, name=f"inv_sums{g}", tag=f"table{freed}")
-            else:
-                inv_sums = work.tile([ROWS, size], F32, name=f"inv_sums{g}")
+        def finish(g, freed):
+            probs = work.tile([ROWS, GROUP_SIZES[g] * KEYS], F32, name=f"probs{g}")
+            tag = f"inv_sums{g}" if freed is None else f"table{freed}"
+            inv_sums = work.tile([ROWS, GROUP_SIZES[g]], F32, name=f"inv_sums{g}", tag=tag)
             nc.vector.reciprocal(inv_sums[:], sums[g][:])
-            for i in range(size):
+            for i in range(GROUP_SIZES[g]):
                 keys = slice(i * KEYS, (i + 1) * KEYS)
-                nc.scalar.activation(
-                    probs[:, keys], powers[g][:, keys], COPY, scale=inv_sums[:, i : i + 1]
-                )
-            columns = slice(FIRST_QUERY[g] * KEYS, (FIRST_QUERY[g] + size) * KEYS)
+                if g >= FIRST_SCALED_BY_VECTOR:
+                    nc.vector.tensor_scalar_mul(
+                        probs[:, keys], powers[g][:, keys], inv_sums[:, i : i + 1]
+                    )
+                else:
+                    nc.scalar.activation(
+                        probs[:, keys], powers[g][:, keys], COPY, scale=inv_sums[:, i : i + 1]
+                    )
+            columns = slice(FIRST_QUERY[g] * KEYS, FIRST_QUERY[g + 1] * KEYS)
             nc.sync.dma_start(out[:, columns], probs[:])
 
-        for g in range(len(GROUP_SIZES)):
-            start_group(g)
+        last_group = len(GROUP_SIZES) - 1
+        for g in range(last_group + 1):
+            for t in range(FIRST_QUERY[g], FIRST_QUERY[g + 1]):
+                gather(g, t)
+            exponentials(g)
             if g > 0:
-                finish_group(g - 1)
-        finish_group(len(GROUP_SIZES) - 1)
+                finish(g - 1, t)
+        finish(last_group, None)

@@ -14,13 +14,13 @@ QUERIES = 32
 KEYS = 128
 OFFSET_COLS = KEYS // 16
 
-GROUP_SIZES = (5, 5, 5, 5, 5, 3, 2, 1, 1)
+GROUP_SIZES = (3, 5, 6, 6, 5, 3, 2, 1, 1)
 assert sum(GROUP_SIZES) == QUERIES
 FIRST_QUERY = [sum(GROUP_SIZES[:g]) for g in range(len(GROUP_SIZES) + 1)]
 
 FIRST_SCALED_BY_VECTOR = 6
 
-PIECE_STARTS = (0, 2, 5, 13, 21, 29)
+PIECE_STARTS = (0, 3, 8, 14, 20, 29)
 
 
 def tile_ngrammultiheadattention_kernel(tc, x, scores, offs, out):

import concourse.mybir as mybir

F32 = mybir.dt.float32
U16 = mybir.dt.uint16
ADD = mybir.AluOpType.add
MAX = mybir.AluOpType.max
EXP = mybir.ActivationFunctionType.Exp
COPY = mybir.ActivationFunctionType.Copy
X_AXIS = mybir.AxisListType.X

ROWS = 128
BUCKETS = 256
QUERIES = 32
KEYS = 128
OFFSET_COLS = KEYS // 16

GROUP_SIZES = (3, 5, 6, 6, 5, 3, 2, 1, 1)
assert sum(GROUP_SIZES) == QUERIES
FIRST_QUERY = [sum(GROUP_SIZES[:g]) for g in range(len(GROUP_SIZES) + 1)]

FIRST_SCALED_BY_VECTOR = 6

PIECE_STARTS = (0, 3, 8, 14, 20, 29)


def tile_ngrammultiheadattention_kernel(tc, x, scores, offs, out):
    nc = tc.nc
    piece_ends = PIECE_STARTS[1:] + (QUERIES,)
    with (
        tc.tile_pool(name="held", bufs=1) as held,
        tc.tile_pool(name="work", bufs=1) as work,
    ):
        offsets = held.tile([ROWS, QUERIES * OFFSET_COLS], U16, name="offsets")
        nc.sync.dma_start(offsets[:], offs)

        tables = []
        addends = []
        for t in range(QUERIES):
            if t in PIECE_STARTS:
                t_end = piece_ends[PIECE_STARTS.index(t)]
                loaded = work.tile([ROWS, (t_end - t) * KEYS], F32, name=f"scores{t}")
                nc.sync.dma_start(loaded[:], scores[:, t * KEYS : t_end * KEYS])
                for i in range(t_end - t):
                    addends.append(loaded[:, i * KEYS : (i + 1) * KEYS])
            table = work.tile([ROWS, BUCKETS], F32, name=f"table{t}")
            nc.sync.dma_start(table[:], x[t, :, :])
            tables.append(table)

        logits = []
        powers = []
        sums = []
        for g, size in enumerate(GROUP_SIZES):
            logits.append(work.tile([ROWS, size * KEYS], F32, name=f"logits{g}"))
            powers.append(work.tile([ROWS, size * KEYS], F32, name=f"powers{g}"))
            sums.append(work.tile([ROWS, size], F32, name=f"sums{g}"))

        def gather(g, t):
            i = t - FIRST_QUERY[g]
            piece = offsets[:, t * OFFSET_COLS : (t + 1) * OFFSET_COLS]
            nc.vector.tensor_tensor(
                logits[g][:, i * KEYS : (i + 1) * KEYS],
                tables[t][:].indirect(piece),
                addends[t],
                ADD,
            )

        def exponentials(g):
            neg_max = work.tile([ROWS, GROUP_SIZES[g]], F32, name=f"neg_max{g}")
            nc.vector.tensor_reduce(
                neg_max[:],
                logits[g][:].rearrange("c (q k) -> c q k", k=KEYS),
                X_AXIS,
                MAX,
                negate=True,
            )
            for i in range(GROUP_SIZES[g]):
                keys = slice(i * KEYS, (i + 1) * KEYS)
                nc.scalar.activation(
                    powers[g][:, keys],
                    logits[g][:, keys],
                    EXP,
                    bias=neg_max[:, i : i + 1],
                    accum_out=sums[g][:, i : i + 1],
                )

        def finish(g, freed):
            probs = work.tile([ROWS, GROUP_SIZES[g] * KEYS], F32, name=f"probs{g}")
            tag = f"inv_sums{g}" if freed is None else f"table{freed}"
            inv_sums = work.tile([ROWS, GROUP_SIZES[g]], F32, name=f"inv_sums{g}", tag=tag)
            nc.vector.reciprocal(inv_sums[:], sums[g][:])
            for i in range(GROUP_SIZES[g]):
                keys = slice(i * KEYS, (i + 1) * KEYS)
                if g >= FIRST_SCALED_BY_VECTOR:
                    nc.vector.tensor_scalar_mul(
                        probs[:, keys], powers[g][:, keys], inv_sums[:, i : i + 1]
                    )
                else:
                    nc.scalar.activation(
                        probs[:, keys], powers[g][:, keys], COPY, scale=inv_sums[:, i : i + 1]
                    )
            columns = slice(FIRST_QUERY[g] * KEYS, FIRST_QUERY[g + 1] * KEYS)
            nc.sync.dma_start(out[:, columns], probs[:])

        last_group = len(GROUP_SIZES) - 1
        for g in range(last_group + 1):
            for t in range(FIRST_QUERY[g], FIRST_QUERY[g + 1]):
                gather(g, t)
            exponentials(g)
            if g > 0:
                finish(g - 1, t)
        finish(last_group, None)
